import numpy as np
import ml_dtypes


def mxq(x, axis, fmt="e4m3"):
    dtype, down = {"e4m3": (ml_dtypes.float8_e4m3fn, 7), "e5m2": (ml_dtypes.float8_e5m2, 14)}[fmt]
    v = np.moveaxis(np.asarray(x, np.float32).astype(ml_dtypes.bfloat16).astype(np.float64), axis, -1)
    blocks = v.reshape(v.shape[:-1] + (-1, 32))
    amax = np.abs(blocks).max(-1, keepdims=True)
    byte = np.maximum(np.where(amax > 0, np.frexp(amax)[1] - 1 + 127, 0) - down, 1)
    scale = np.exp2(byte - 127.0)
    codes = (blocks / scale).astype(np.float32).astype(dtype).astype(np.float64)
    return np.moveaxis((codes * scale).reshape(v.shape), -1, axis)


WIDE = False


def mx_kscale(k):
    if not WIDE:
        return np.ones(k)
    levels = np.array([10, -10, 5, -5, 0])
    a = np.random.permutation(np.resize(levels, k // 512 * 4)).reshape(k // 512, 4)
    idx = np.arange(k)
    return np.exp2(a[idx // 512, idx % 128 // 32])


BF16 = ml_dtypes.bfloat16


def bf(x):
    return np.asarray(x, np.float32).astype(BF16)


def f64(x):
    return np.asarray(x).astype(np.float64)


B, S, D, H, F = 3, 256, 1024, 16, 3072
EPS = 1e-6


def layernorm(v, gamma, beta):
    mu = v.mean(-1, keepdims=True)
    var = np.square(v - mu).mean(-1, keepdims=True)
    return gamma * (v - mu) * (1.0 / np.sqrt(var + EPS)) + beta


def setup_inputs():
    t = mx_kscale(F)
    n = np.random.standard_normal
    return {"h_attn": bf(n((B, S, D))),
            "w1": bf(n((D, F)) / np.sqrt(D) * t),
            "b1": bf(0.2 * n(F) * t),
            "w2": bf(n((F, D)) / np.sqrt(F) / t[:, None]),
            "b2": bf(0.3 + 0.2 * n(D)),
            "g2": bf(1.0 + 0.1 * n(D)),
            "be2": bf(0.2 * n(D))}


def reference(h_attn, w1, b1, w2, b2, g2, be2):
    y = f64(h_attn)
    h = np.maximum((mxq(y, 2, "e4m3") @ mxq(f64(w1), 0, "e4m3")) + f64(b1), 0.0)
    ffn = (mxq(h, 2, "e4m3") @ mxq(f64(w2), 0, "e4m3")) + f64(b2)
    return layernorm(y + ffn, f64(g2), f64(be2))

@@ -1,0 +1,299 @@
+from contextlib import ExitStack
+
+import concourse.mybir as mybir
+from concourse.masks import make_identity
+
+F32 = mybir.dt.float32
+BF16 = mybir.dt.bfloat16
+U32 = mybir.dt.uint32
+U8 = mybir.dt.uint8
+FP8X4 = mybir.dt.float8_e4m3fn_x4
+ALU = mybir.AluOpType
+ACT = mybir.ActivationFunctionType
+
+P = 128
+PACK = 4
+K_PASS = P * PACK
+BANK = 512
+
+TOKENS = 768
+D_MODEL = 1024
+D_HIDDEN = 3072
+EPS = 1e-6
+
+TOKEN_TILES = TOKENS // P
+HIDDEN_TILES = D_HIDDEN // P
+PASSES_1 = D_MODEL // K_PASS
+PASSES_2 = D_HIDDEN // K_PASS
+
+UNIT_COLS = 1024
+W1_UNITS = PASSES_1 * (D_HIDDEN // UNIT_COLS)
+W2_UNITS = PASSES_2
+UNITS = W1_UNITS + W2_UNITS
+RAW_BUFS = 5
+
+SCALAR_COLS = 192
+VECTOR_COLS = UNIT_COLS - SCALAR_COLS
+
+FLOPS = 2 * 2 * TOKENS * D_MODEL * D_HIDDEN
+
+
+def regrouped(dst, src):
+    return (
+        dst.rearrange("p (c i) t -> p c t i", i=4),
+        src.rearrange("p t (c i) -> p c t i", i=4),
+    )
+
+
+def tile_decoderlayer_pb_kernel(tc, h_attn, w1, b1, w2, b2, g2, be2, out):
+    nc = tc.nc
+    x_rows = h_attn.flatten_outer_dims()
+    out_rows = out.flatten_outer_dims()
+
+    with ExitStack() as whole:
+        keep = whole.enter_context(tc.tile_pool(name="keep", bufs=1))
+        psum = whole.enter_context(tc.psum_pool(name="psum", bufs=8))
+
+        ident_f32 = keep.tile([P, P], F32, name="ident_f32")
+        ident_bf = keep.tile([P, P], BF16, name="ident_bf")
+        ones_bf = keep.tile([P, P], BF16, name="ones_bf")
+        eps_col = keep.tile([P, 1], F32, name="eps_col")
+        b1_cols = keep.tile([P, P], F32, name="b1_cols")
+        x_codes = keep.tile([P, PASSES_1, TOKENS], U32, name="x_codes", align_bytes=64)
+        x_scales = keep.tile([P, PASSES_1, TOKENS], U8, name="x_scales", align_bytes=64)
+        w1_codes = keep.tile([P, PASSES_1, D_HIDDEN], U32, name="w1_codes", align_bytes=64)
+        w1_scales = keep.tile([P, PASSES_1, D_HIDDEN], U8, name="w1_scales", align_bytes=64)
+        w2_codes = keep.tile([P, PASSES_2, D_MODEL], U32, name="w2_codes", align_bytes=64)
+        w2_scales = keep.tile([P, PASSES_2, D_MODEL], U8, name="w2_scales", align_bytes=64)
+        hidden = keep.tile([P, HIDDEN_TILES, TOKENS], BF16, name="hidden")
+        resid = keep.tile([P, TOKEN_TILES, D_MODEL], F32, name="resid")
+        gain_bc = keep.tile([P, D_MODEL], BF16, name="gain_bc")
+        shift_bc = keep.tile([P, D_MODEL], BF16, name="shift_bc")
+
+        make_identity(nc, ident_f32[:])
+        make_identity(nc, ident_bf[:])
+        nc.vector.memset(ones_bf[:], 1.0)
+        nc.vector.memset(eps_col[:], EPS)
+        warm = keep.tile([P, 1], F32, name="warm")
+        nc.scalar.activation(out=warm[:], in_=eps_col[:], func=ACT.Sqrt)
+
+        with ExitStack() as part1:
+            raw_pool = part1.enter_context(tc.tile_pool(name="raw", bufs=RAW_BUFS))
+            grouped_pool = part1.enter_context(tc.tile_pool(name="grouped", bufs=3))
+            head = part1.enter_context(tc.tile_pool(name="head", bufs=1))
+
+            x_sb = head.tile([P, TOKEN_TILES, D_MODEL], BF16, name="x_sb")
+            b2_rows = head.tile([P, D_MODEL], BF16, name="b2_rows")
+            b1_rows = head.tile([P, P], BF16, name="b1_rows")
+
+            raw_units = {}
+            grouped_units = {}
+
+            def load_unit(n):
+                raw = raw_pool.tile([P, PACK, UNIT_COLS], BF16, name="raw")
+                raw_units[n] = raw
+                if n < W1_UNITS:
+                    c, g = divmod(n, PASSES_1)
+                    cols = slice(c * UNIT_COLS, (c + 1) * UNIT_COLS)
+                    for u in range(2):
+                        k0 = g * K_PASS + u * 2 * P
+                        nc.sync.dma_start(
+                            out=raw[:, 2 * u : 2 * u + 2, :],
+                            in_=w1[k0 : k0 + 2 * P, cols].rearrange("(p e) n -> p e n", e=2),
+                        )
+                else:
+                    k0 = (n - W1_UNITS) * K_PASS
+                    nc.sync.dma_start(
+                        out=raw[:], in_=w2[k0 : k0 + K_PASS, :].rearrange("(t p) n -> p t n", p=P)
+                    )
+
+            def regroup_unit(n):
+                raw = raw_units[n]
+                grouped = grouped_pool.tile([P, UNIT_COLS, PACK], BF16, name="grouped", align_bytes=64)
+                grouped_units[n] = grouped
+                dst, src = regrouped(grouped[:, :VECTOR_COLS, :], raw[:, :, :VECTOR_COLS])
+                nc.vector.tensor_copy(out=dst, in_=src)
+                dst, src = regrouped(grouped[:, VECTOR_COLS:, :], raw[:, :, VECTOR_COLS:])
+                nc.scalar.copy(out=dst, in_=src)
+
+            def quantise_unit(n):
+                grouped = grouped_units[n]
+                if n < W1_UNITS:
+                    c, g = divmod(n, PASSES_1)
+                    cols = slice(c * UNIT_COLS, (c + 1) * UNIT_COLS)
+                    codes, scales = w1_codes[:, g, cols], w1_scales[:, g, cols]
+                else:
+                    codes, scales = w2_codes[:, n - W1_UNITS, :], w2_scales[:, n - W1_UNITS, :]
+                nc.vector.quantize_mx(
+                    out=codes.bitcast(FP8X4),
+                    scales=scales,
+                    in_=grouped[:].rearrange("p w t -> p (w t)"),
+                )
+
+            def quantise_tokens():
+                for j in range(TOKEN_TILES // 2):
+                    pairs = head.tile([P, PASSES_1, 2 * P, 2], F32, name="pairs%d" % j, align_bytes=64)
+                    for a in range(2):
+                        i = 2 * j + a
+                        words = x_sb[:, i, :].bitcast(F32)
+                        flipped = psum.tile([P, 2 * PASSES_1, P], F32, name="flipped", tag="bank")
+                        for q in range(2 * PASSES_1):
+                            nc.tensor.transpose(flipped[:, q, :], words[:, q * P : (q + 1) * P], ident_f32[:])
+                        nc.scalar.copy(
+                            out=pairs[:, :, a * P : (a + 1) * P, :],
+                            in_=flipped[:].rearrange("p (g u) w -> p g w u", u=2),
+                        )
+                    toks = slice(j * 2 * P, (j + 1) * 2 * P)
+                    for g in range(PASSES_1):
+                        nc.vector.quantize_mx(
+                            out=x_codes[:, g, toks].bitcast(FP8X4),
+                            scales=x_scales[:, g, toks],
+                            in_=pairs[:, g].bitcast(BF16).rearrange("p w t -> p (w t)"),
+                        )
+
+            def hidden_pair(q):
+                rest = psum.tile([P, 2, TOKENS - BANK], F32, name="rest", tag="bank")
+                pieces = []
+                for a in range(2):
+                    f = 2 * q + a
+                    main = psum.tile([P, BANK], F32, name="main", tag="bank")
+                    pieces.append((f, main[:], slice(0, BANK)))
+                    pieces.append((f, rest[:, a, :], slice(BANK, TOKENS)))
+                for f, acc, toks in pieces:
+                    cols = slice(f * P, (f + 1) * P)
+                    for g in range(PASSES_1):
+                        nc.tensor.matmul_mx(
+                            out=acc,
+                            lhsT=w1_codes[:, g, cols].bitcast(FP8X4),
+                            lhsT_scale=w1_scales[:, g, cols],
+                            rhs=x_codes[:, g, toks].bitcast(FP8X4),
+                            rhs_scale=x_scales[:, g, toks],
+                            start=(g == 0),
+                            stop=(g == PASSES_1 - 1),
+                        )
+                for f, acc, toks in pieces:
+                    nc.scalar.activation(
+                        out=hidden[:, f, toks], in_=acc, func=ACT.Relu, bias=b1_cols[:, f : f + 1], scale=1.0
+                    )
+
+            def residual_piece(n):
+                i, half = divmod(n, 2)
+                cols = slice(half * BANK, (half + 1) * BANK)
+                acc = psum.tile([P, BANK], F32, name="resid_acc", tag="bank")
+                nc.tensor.matmul(out=acc[:], lhsT=ident_bf[:], rhs=x_sb[:, i, cols], start=True, stop=False)
+                nc.tensor.matmul(out=acc[:], lhsT=ones_bf[:], rhs=b2_rows[:, cols], start=False, stop=True)
+                nc.scalar.copy(out=resid[:, i, cols], in_=acc[:])
+
+            nc.vector.memset(b1_rows[:], 0.0)
+            nc.vector.memset(b2_rows[:], 0.0)
+            nc.scalar.dma_start(out=b1_rows[:HIDDEN_TILES, :], in_=b1.rearrange("(f p) -> f p", p=P))
+            nc.scalar.dma_start(out=b2_rows[0:1, :], in_=b2.rearrange("(o d) -> o d", o=1))
+
+            load_unit(0)
+            load_unit(1)
+            for j in range(TOKEN_TILES // 2):
+                nc.sync.dma_start(
+                    out=x_sb[:, 2 * j : 2 * j + 2, :],
+                    in_=x_rows[j * 2 * P : (j + 1) * 2 * P, :].rearrange("(a p) d -> p a d", p=P),
+                )
+            for n in range(2, RAW_BUFS):
+                load_unit(n)
+
+            regroup_unit(0)
+            load_unit(RAW_BUFS)
+            regroup_unit(1)
+            load_unit(RAW_BUFS + 1)
+            quantise_unit(0)
+
+            b1_flipped = psum.tile([P, P], BF16, name="b1_flipped", tag="bank")
+            nc.tensor.transpose(b1_flipped[:], b1_rows[:], ident_bf[:])
+            nc.scalar.copy(out=b1_cols[:], in_=b1_flipped[:])
+
+            quantise_tokens()
+
+            for n in range(2, UNITS + 2):
+                if n < UNITS:
+                    regroup_unit(n)
+                    if n + RAW_BUFS < UNITS:
+                        load_unit(n + RAW_BUFS)
+                if n - 1 < UNITS:
+                    quantise_unit(n - 1)
+                hidden_pair(n - 2)
+                residual_piece(n - 2)
+
+            nc.sync.dma_start(out=gain_bc[:], in_=g2.partition_broadcast(P))
+            nc.sync.dma_start(out=shift_bc[:], in_=be2.partition_broadcast(P))
+
+        with ExitStack() as part2:
+            work = part2.enter_context(tc.tile_pool(name="work", bufs=3, reuse_waits="tile"))
+            small = part2.enter_context(tc.tile_pool(name="small", bufs=4, reuse_waits="tile"))
+
+            for i in range(TOKEN_TILES):
+                toks = slice(i * P, (i + 1) * P)
+
+                h_grouped = work.tile([P, PASSES_2, P, PACK], BF16, name="h_grouped", align_bytes=64)
+                for g in range(PASSES_2):
+                    dst, src = regrouped(h_grouped[:, g], hidden[:, PACK * g : PACK * (g + 1), toks])
+                    nc.scalar.copy(out=dst, in_=src)
+                h_codes = work.tile([P, PASSES_2, P], U32, name="h_codes", align_bytes=64)
+                h_scales = work.tile([P, PASSES_2, P], U8, name="h_scales", align_bytes=64)
+                for g0, g1 in ((0, 4), (4, 6)):
+                    nc.vector.quantize_mx(
+                        out=h_codes[:, g0:g1, :].rearrange("p g w -> p (g w)").bitcast(FP8X4),
+                        scales=h_scales[:, g0:g1, :].rearrange("p g w -> p (g w)"),
+                        in_=h_grouped[:, g0:g1].rearrange("p g w t -> p (g w t)"),
+                    )
+
+                r = work.tile([P, D_MODEL], F32, name="r")
+                row_sum = small.tile([P, 2], F32, name="row_sum")
+                for half in range(2):
+                    cols = slice(half * BANK, (half + 1) * BANK)
+                    acc = psum.tile([P, BANK], F32, name="ffn", tag="bank")
+                    for g in range(PASSES_2):
+                        nc.tensor.matmul_mx(
+                            out=acc[:],
+                            lhsT=h_codes[:, g, :].bitcast(FP8X4),
+                            lhsT_scale=h_scales[:, g, :],
+                            rhs=w2_codes[:, g, cols].bitcast(FP8X4),
+                            rhs_scale=w2_scales[:, g, cols],
+                            start=(g == 0),
+                            stop=(g == PASSES_2 - 1),
+                        )
+                    nc.vector.scalar_tensor_tensor(
+                        out=r[:, cols],
+                        in0=acc[:],
+                        scalar=0.0,
+                        in1=resid[:, i, cols],
+                        op0=ALU.add,
+                        op1=ALU.add,
+                        accum_out=row_sum[:, half : half + 1],
+                    )
+
+                neg_mean = small.tile([P, 1], F32, name="neg_mean")
+                nc.vector.tensor_scalar(
+                    out=neg_mean[:],
+                    in0=row_sum[:, 0:1],
+                    scalar1=row_sum[:, 1:2],
+                    scalar2=-1.0 / D_MODEL,
+                    op0=ALU.add,
+                    op1=ALU.mult,
+                )
+                squares = work.tile([P, D_MODEL], BF16, name="squares")
+                sum_sq = small.tile([P, 1], F32, name="sum_sq")
+                nc.scalar.activation(
+                    out=squares[:], in_=r[:], func=ACT.Square, bias=neg_mean[:], scale=1.0, accum_out=sum_sq[:]
+                )
+                std = small.tile([P, 1], F32, name="std")
+                nc.scalar.activation(out=std[:], in_=sum_sq[:], func=ACT.Sqrt, bias=eps_col[:], scale=1.0 / D_MODEL)
+                rstd = small.tile([P, 1], F32, name="rstd")
+                nc.vector.reciprocal(out=rstd[:], in_=std[:])
+
+                centred = work.tile([P, D_MODEL], F32, name="centred")
+                nc.vector.scalar_tensor_tensor(
+                    out=centred[:], in0=r[:], scalar=neg_mean[:], in1=gain_bc[:], op0=ALU.add, op1=ALU.mult
+                )
+                normed = work.tile([P, D_MODEL], F32, name="normed")
+                nc.vector.scalar_tensor_tensor(
+                    out=normed[:], in0=centred[:], scalar=rstd[:], in1=shift_bc[:], op0=ALU.mult, op1=ALU.add
+                )
+                nc.sync.dma_start(out=out_rows[toks, :], in_=normed[:])

@@ -23,6 +23,7 @@ EPS = 1e-6
 
 TOKEN_TILES = TOKENS // P
 HIDDEN_TILES = D_HIDDEN // P
+HIDDEN_PAIRS = HIDDEN_TILES // 2
 PASSES_1 = D_MODEL // K_PASS
 PASSES_2 = D_HIDDEN // K_PASS
 
@@ -32,8 +33,17 @@ W2_UNITS = PASSES_2
 UNITS = W1_UNITS + W2_UNITS
 RAW_BUFS = 5
 
-SCALAR_COLS = 192
+SCALAR_COLS = 160
 VECTOR_COLS = UNIT_COLS - SCALAR_COLS
+
+FIRST_PAIR_STEP = 2
+PAIRS_A_STEP = 2
+H_REGROUP_STEP = FIRST_PAIR_STEP + HIDDEN_PAIRS // PAIRS_A_STEP
+H_QUANTISE_STEP = H_REGROUP_STEP + 2
+PRODUCT_STEP = UNITS
+CENTRE_STEP = PRODUCT_STEP + 1
+STORE_STEP = CENTRE_STEP + 1
+LAST_STEP = STORE_STEP + TOKEN_TILES - 1
 
 FLOPS = 2 * 2 * TOKENS * D_MODEL * D_HIDDEN
 
@@ -52,6 +62,8 @@ def tile_decoderlayer_pb_kernel(tc, h_attn, w1, b1, w2, b2, g2, be2, out):
 
     with ExitStack() as whole:
         keep = whole.enter_context(tc.tile_pool(name="keep", bufs=1))
+        raw_pool = whole.enter_context(tc.tile_pool(name="raw", bufs=RAW_BUFS))
+        grouped_pool = whole.enter_context(tc.tile_pool(name="grouped", bufs=3))
         psum = whole.enter_context(tc.psum_pool(name="psum", bufs=8))
 
         ident_f32 = keep.tile([P, P], F32, name="ident_f32")
@@ -59,10 +71,6 @@ def tile_decoderlayer_pb_kernel(tc, h_attn, w1, b1, w2, b2, g2, be2, out):
         ones_bf = keep.tile([P, P], BF16, name="ones_bf")
         eps_col = keep.tile([P, 1], F32, name="eps_col")
         b1_cols = keep.tile([P, P], F32, name="b1_cols")
-        x_codes = keep.tile([P, PASSES_1, TOKENS], U32, name="x_codes", align_bytes=64)
-        x_scales = keep.tile([P, PASSES_1, TOKENS], U8, name="x_scales", align_bytes=64)
-        w1_codes = keep.tile([P, PASSES_1, D_HIDDEN], U32, name="w1_codes", align_bytes=64)
-        w1_scales = keep.tile([P, PASSES_1, D_HIDDEN], U8, name="w1_scales", align_bytes=64)
         w2_codes = keep.tile([P, PASSES_2, D_MODEL], U32, name="w2_codes", align_bytes=64)
         w2_scales = keep.tile([P, PASSES_2, D_MODEL], U8, name="w2_scales", align_bytes=64)
         hidden = keep.tile([P, HIDDEN_TILES, TOKENS], BF16, name="hidden")
@@ -77,79 +85,86 @@ def tile_decoderlayer_pb_kernel(tc, h_attn, w1, b1, w2, b2, g2, be2, out):
         warm = keep.tile([P, 1], F32, name="warm")
         nc.scalar.activation(out=warm[:], in_=eps_col[:], func=ACT.Sqrt)
 
-        with ExitStack() as part1:
-            raw_pool = part1.enter_context(tc.tile_pool(name="raw", bufs=RAW_BUFS))
-            grouped_pool = part1.enter_context(tc.tile_pool(name="grouped", bufs=3))
-            head = part1.enter_context(tc.tile_pool(name="head", bufs=1))
+        raw_units = {}
+        grouped_units = {}
 
-            x_sb = head.tile([P, TOKEN_TILES, D_MODEL], BF16, name="x_sb")
-            b2_rows = head.tile([P, D_MODEL], BF16, name="b2_rows")
-            b1_rows = head.tile([P, P], BF16, name="b1_rows")
-
-            raw_units = {}
-            grouped_units = {}
-
-            def load_unit(n):
-                raw = raw_pool.tile([P, PACK, UNIT_COLS], BF16, name="raw")
-                raw_units[n] = raw
-                if n < W1_UNITS:
-                    c, g = divmod(n, PASSES_1)
-                    cols = slice(c * UNIT_COLS, (c + 1) * UNIT_COLS)
-                    for u in range(2):
-                        k0 = g * K_PASS + u * 2 * P
-                        nc.sync.dma_start(
-                            out=raw[:, 2 * u : 2 * u + 2, :],
-                            in_=w1[k0 : k0 + 2 * P, cols].rearrange("(p e) n -> p e n", e=2),
-                        )
-                else:
-                    k0 = (n - W1_UNITS) * K_PASS
+        def load_unit(n):
+            raw = raw_pool.tile([P, PACK, UNIT_COLS], BF16, name="raw")
+            raw_units[n] = raw
+            if n < W1_UNITS:
+                c, g = divmod(n, PASSES_1)
+                cols = slice(c * UNIT_COLS, (c + 1) * UNIT_COLS)
+                for u in range(2):
+                    k0 = g * K_PASS + u * 2 * P
                     nc.sync.dma_start(
-                        out=raw[:], in_=w2[k0 : k0 + K_PASS, :].rearrange("(t p) n -> p t n", p=P)
+                        out=raw[:, 2 * u : 2 * u + 2, :],
+                        in_=w1[k0 : k0 + 2 * P, cols].rearrange("(p e) n -> p e n", e=2),
                     )
+            else:
+                k0 = (n - W1_UNITS) * K_PASS
+                nc.sync.dma_start(
+                    out=raw[:], in_=w2[k0 : k0 + K_PASS, :].rearrange("(t p) n -> p t n", p=P)
+                )
 
-            def regroup_unit(n):
-                raw = raw_units[n]
-                grouped = grouped_pool.tile([P, UNIT_COLS, PACK], BF16, name="grouped", align_bytes=64)
-                grouped_units[n] = grouped
-                dst, src = regrouped(grouped[:, :VECTOR_COLS, :], raw[:, :, :VECTOR_COLS])
-                nc.vector.tensor_copy(out=dst, in_=src)
-                dst, src = regrouped(grouped[:, VECTOR_COLS:, :], raw[:, :, VECTOR_COLS:])
-                nc.scalar.copy(out=dst, in_=src)
+        def regroup_unit(n):
+            raw = raw_units[n]
+            grouped = grouped_pool.tile([P, UNIT_COLS, PACK], BF16, name="grouped", align_bytes=64)
+            grouped_units[n] = grouped
+            dst, src = regrouped(grouped[:, :VECTOR_COLS, :], raw[:, :, :VECTOR_COLS])
+            nc.vector.tensor_copy(out=dst, in_=src)
+            dst, src = regrouped(grouped[:, VECTOR_COLS:, :], raw[:, :, VECTOR_COLS:])
+            nc.scalar.copy(out=dst, in_=src)
+            if n + RAW_BUFS < UNITS:
+                load_unit(n + RAW_BUFS)
 
-            def quantise_unit(n):
-                grouped = grouped_units[n]
-                if n < W1_UNITS:
-                    c, g = divmod(n, PASSES_1)
-                    cols = slice(c * UNIT_COLS, (c + 1) * UNIT_COLS)
-                    codes, scales = w1_codes[:, g, cols], w1_scales[:, g, cols]
-                else:
-                    codes, scales = w2_codes[:, n - W1_UNITS, :], w2_scales[:, n - W1_UNITS, :]
-                nc.vector.quantize_mx(
-                    out=codes.bitcast(FP8X4),
-                    scales=scales,
-                    in_=grouped[:].rearrange("p w t -> p (w t)"),
+        def quantise_unit(n, codes, scales):
+            nc.vector.quantize_mx(
+                out=codes.bitcast(FP8X4),
+                scales=scales,
+                in_=grouped_units[n][:].rearrange("p w t -> p (w t)"),
+            )
+
+        with tc.tile_pool(name="early", bufs=1) as early:
+            x_sb = early.tile([P, TOKEN_TILES, D_MODEL], BF16, name="x_sb")
+            b2_rows = early.tile([P, D_MODEL], BF16, name="b2_rows")
+            b1_rows = early.tile([P, P], BF16, name="b1_rows")
+            x_codes = early.tile([P, PASSES_1, TOKENS], U32, name="x_codes", align_bytes=64)
+            x_scales = early.tile([P, PASSES_1, TOKENS], U8, name="x_scales", align_bytes=64)
+            w1_codes = early.tile([P, PASSES_1, D_HIDDEN], U32, name="w1_codes", align_bytes=64)
+            w1_scales = early.tile([P, PASSES_1, D_HIDDEN], U8, name="w1_scales", align_bytes=64)
+            x_grouped = early.tile([P, PASSES_1, TOKENS, 2], F32, name="x_grouped", align_bytes=64)
+
+            def quantise_w1_unit(n):
+                c, g = divmod(n, PASSES_1)
+                cols = slice(c * UNIT_COLS, (c + 1) * UNIT_COLS)
+                quantise_unit(n, w1_codes[:, g, cols], w1_scales[:, g, cols])
+
+            def transpose_tokens(i):
+                words = x_sb[:, i, :].bitcast(F32)
+                flipped = psum.tile([P, 2 * PASSES_1, P], F32, name="flipped", tag="bank")
+                for q in range(2 * PASSES_1):
+                    nc.tensor.transpose(flipped[:, q, :], words[:, q * P : (q + 1) * P], ident_f32[:])
+                nc.scalar.copy(
+                    out=x_grouped[:, :, i * P : (i + 1) * P, :],
+                    in_=flipped[:].rearrange("p (g u) w -> p g w u", u=2),
                 )
 
             def quantise_tokens():
-                for j in range(TOKEN_TILES // 2):
-                    pairs = head.tile([P, PASSES_1, 2 * P, 2], F32, name="pairs%d" % j, align_bytes=64)
-                    for a in range(2):
-                        i = 2 * j + a
-                        words = x_sb[:, i, :].bitcast(F32)
-                        flipped = psum.tile([P, 2 * PASSES_1, P], F32, name="flipped", tag="bank")
-                        for q in range(2 * PASSES_1):
-                            nc.tensor.transpose(flipped[:, q, :], words[:, q * P : (q + 1) * P], ident_f32[:])
-                        nc.scalar.copy(
-                            out=pairs[:, :, a * P : (a + 1) * P, :],
-                            in_=flipped[:].rearrange("p (g u) w -> p g w u", u=2),
-                        )
-                    toks = slice(j * 2 * P, (j + 1) * 2 * P)
+                for j in range(TOKENS // 256):
+                    toks = slice(j * 256, (j + 1) * 256)
                     for g in range(PASSES_1):
                         nc.vector.quantize_mx(
                             out=x_codes[:, g, toks].bitcast(FP8X4),
                             scales=x_scales[:, g, toks],
-                            in_=pairs[:, g].bitcast(BF16).rearrange("p w t -> p (w t)"),
+                            in_=x_grouped[:, g, toks, :].bitcast(BF16).rearrange("p w t -> p (w t)"),
                         )
+
+            def residual_piece(i, half):
+                cols = slice(half * BANK, (half + 1) * BANK)
+                acc = psum.tile([P, BANK], F32, name="resid_acc", tag="bank")
+                nc.tensor.matmul(out=acc[:], lhsT=ident_bf[:], rhs=x_sb[:, i, cols], start=True, stop=False)
+                nc.tensor.matmul(out=acc[:], lhsT=ones_bf[:], rhs=b2_rows[:, cols], start=False, stop=True)
+                nc.scalar.copy(out=resid[:, i, cols], in_=acc[:])
 
             def hidden_pair(q):
                 rest = psum.tile([P, 2, TOKENS - BANK], F32, name="rest", tag="bank")
@@ -176,124 +191,146 @@ def tile_decoderlayer_pb_kernel(tc, h_attn, w1, b1, w2, b2, g2, be2, out):
                         out=hidden[:, f, toks], in_=acc, func=ACT.Relu, bias=b1_cols[:, f : f + 1], scale=1.0
                     )
 
-            def residual_piece(n):
-                i, half = divmod(n, 2)
-                cols = slice(half * BANK, (half + 1) * BANK)
-                acc = psum.tile([P, BANK], F32, name="resid_acc", tag="bank")
-                nc.tensor.matmul(out=acc[:], lhsT=ident_bf[:], rhs=x_sb[:, i, cols], start=True, stop=False)
-                nc.tensor.matmul(out=acc[:], lhsT=ones_bf[:], rhs=b2_rows[:, cols], start=False, stop=True)
-                nc.scalar.copy(out=resid[:, i, cols], in_=acc[:])
-
             nc.vector.memset(b1_rows[:], 0.0)
             nc.vector.memset(b2_rows[:], 0.0)
             nc.scalar.dma_start(out=b1_rows[:HIDDEN_TILES, :], in_=b1.rearrange("(f p) -> f p", p=P))
             nc.scalar.dma_start(out=b2_rows[0:1, :], in_=b2.rearrange("(o d) -> o d", o=1))
 
-            load_unit(0)
-            load_unit(1)
             for j in range(TOKEN_TILES // 2):
                 nc.sync.dma_start(
                     out=x_sb[:, 2 * j : 2 * j + 2, :],
                     in_=x_rows[j * 2 * P : (j + 1) * 2 * P, :].rearrange("(a p) d -> p a d", p=P),
                 )
-            for n in range(2, RAW_BUFS):
+            for n in range(RAW_BUFS):
                 load_unit(n)
-
-            regroup_unit(0)
-            load_unit(RAW_BUFS)
-            regroup_unit(1)
-            load_unit(RAW_BUFS + 1)
-            quantise_unit(0)
 
             b1_flipped = psum.tile([P, P], BF16, name="b1_flipped", tag="bank")
             nc.tensor.transpose(b1_flipped[:], b1_rows[:], ident_bf[:])
             nc.scalar.copy(out=b1_cols[:], in_=b1_flipped[:])
 
+            for i in range(TOKEN_TILES):
+                transpose_tokens(i)
+            regroup_unit(0)
             quantise_tokens()
+            regroup_unit(1)
+            quantise_w1_unit(0)
+            for i in range(TOKEN_TILES):
+                for half in range(2):
+                    residual_piece(i, half)
 
-            for n in range(2, UNITS + 2):
-                if n < UNITS:
-                    regroup_unit(n)
-                    if n + RAW_BUFS < UNITS:
-                        load_unit(n + RAW_BUFS)
-                if n - 1 < UNITS:
-                    quantise_unit(n - 1)
-                hidden_pair(n - 2)
-                residual_piece(n - 2)
+            for n in range(FIRST_PAIR_STEP, H_REGROUP_STEP):
+                regroup_unit(n)
+                if n - 1 < W1_UNITS:
+                    quantise_w1_unit(n - 1)
+                else:
+                    quantise_unit(n - 1, w2_codes[:, n - 1 - W1_UNITS, :], w2_scales[:, n - 1 - W1_UNITS, :])
+                for q in range(PAIRS_A_STEP * (n - FIRST_PAIR_STEP), PAIRS_A_STEP * (n - FIRST_PAIR_STEP + 1)):
+                    hidden_pair(q)
 
+        with tc.tile_pool(name="late", bufs=3, reuse_waits="tile") as late:
             nc.sync.dma_start(out=gain_bc[:], in_=g2.partition_broadcast(P))
             nc.sync.dma_start(out=shift_bc[:], in_=be2.partition_broadcast(P))
 
-        with ExitStack() as part2:
-            work = part2.enter_context(tc.tile_pool(name="work", bufs=3, reuse_waits="tile"))
-            small = part2.enter_context(tc.tile_pool(name="small", bufs=4, reuse_waits="tile"))
+            h_grouped = {}
+            h_codes = {}
+            h_scales = {}
+            ffn = {}
+            neg_mean = {}
+            std = {}
+            centred = {}
 
-            for i in range(TOKEN_TILES):
+            def regroup_hidden(i):
                 toks = slice(i * P, (i + 1) * P)
-
-                h_grouped = work.tile([P, PASSES_2, P, PACK], BF16, name="h_grouped", align_bytes=64)
+                h_grouped[i] = late.tile([P, PASSES_2, P, PACK], BF16, name="h_grouped", align_bytes=64)
                 for g in range(PASSES_2):
-                    dst, src = regrouped(h_grouped[:, g], hidden[:, PACK * g : PACK * (g + 1), toks])
+                    dst, src = regrouped(h_grouped[i][:, g], hidden[:, PACK * g : PACK * (g + 1), toks])
                     nc.scalar.copy(out=dst, in_=src)
-                h_codes = work.tile([P, PASSES_2, P], U32, name="h_codes", align_bytes=64)
-                h_scales = work.tile([P, PASSES_2, P], U8, name="h_scales", align_bytes=64)
+
+            def quantise_hidden(i):
+                h_codes[i] = late.tile([P, PASSES_2, P], U32, name="h_codes", align_bytes=64)
+                h_scales[i] = late.tile([P, PASSES_2, P], U8, name="h_scales", align_bytes=64)
                 for g0, g1 in ((0, 4), (4, 6)):
                     nc.vector.quantize_mx(
-                        out=h_codes[:, g0:g1, :].rearrange("p g w -> p (g w)").bitcast(FP8X4),
-                        scales=h_scales[:, g0:g1, :].rearrange("p g w -> p (g w)"),
-                        in_=h_grouped[:, g0:g1].rearrange("p g w t -> p (g w t)"),
+                        out=h_codes[i][:, g0:g1, :].rearrange("p g w -> p (g w)").bitcast(FP8X4),
+                        scales=h_scales[i][:, g0:g1, :].rearrange("p g w -> p (g w)"),
+                        in_=h_grouped[i][:, g0:g1].rearrange("p g w t -> p (g w t)"),
                     )
 
-                r = work.tile([P, D_MODEL], F32, name="r")
-                row_sum = small.tile([P, 2], F32, name="row_sum")
+            def second_product(i):
+                ffn[i] = []
                 for half in range(2):
                     cols = slice(half * BANK, (half + 1) * BANK)
                     acc = psum.tile([P, BANK], F32, name="ffn", tag="bank")
+                    ffn[i].append(acc)
                     for g in range(PASSES_2):
                         nc.tensor.matmul_mx(
                             out=acc[:],
-                            lhsT=h_codes[:, g, :].bitcast(FP8X4),
-                            lhsT_scale=h_scales[:, g, :],
+                            lhsT=h_codes[i][:, g, :].bitcast(FP8X4),
+                            lhsT_scale=h_scales[i][:, g, :],
                             rhs=w2_codes[:, g, cols].bitcast(FP8X4),
                             rhs_scale=w2_scales[:, g, cols],
                             start=(g == 0),
                             stop=(g == PASSES_2 - 1),
                         )
+
+            def add_and_centre(i):
+                r = late.tile([P, D_MODEL], F32, name="r")
+                row_sum = late.tile([P, 2], F32, name="row_sum")
+                for half in range(2):
+                    cols = slice(half * BANK, (half + 1) * BANK)
                     nc.vector.scalar_tensor_tensor(
                         out=r[:, cols],
-                        in0=acc[:],
+                        in0=ffn[i][half][:],
                         scalar=0.0,
                         in1=resid[:, i, cols],
                         op0=ALU.add,
                         op1=ALU.add,
                         accum_out=row_sum[:, half : half + 1],
                     )
-
-                neg_mean = small.tile([P, 1], F32, name="neg_mean")
+                neg_mean[i] = late.tile([P, 1], F32, name="neg_mean")
                 nc.vector.tensor_scalar(
-                    out=neg_mean[:],
+                    out=neg_mean[i][:],
                     in0=row_sum[:, 0:1],
                     scalar1=row_sum[:, 1:2],
                     scalar2=-1.0 / D_MODEL,
                     op0=ALU.add,
                     op1=ALU.mult,
                 )
-                squares = work.tile([P, D_MODEL], BF16, name="squares")
-                sum_sq = small.tile([P, 1], F32, name="sum_sq")
+                squares = late.tile([P, D_MODEL], BF16, name="squares")
+                sum_sq = late.tile([P, 1], F32, name="sum_sq")
                 nc.scalar.activation(
-                    out=squares[:], in_=r[:], func=ACT.Square, bias=neg_mean[:], scale=1.0, accum_out=sum_sq[:]
+                    out=squares[:], in_=r[:], func=ACT.Square, bias=neg_mean[i][:], scale=1.0, accum_out=sum_sq[:]
                 )
-                std = small.tile([P, 1], F32, name="std")
-                nc.scalar.activation(out=std[:], in_=sum_sq[:], func=ACT.Sqrt, bias=eps_col[:], scale=1.0 / D_MODEL)
-                rstd = small.tile([P, 1], F32, name="rstd")
-                nc.vector.reciprocal(out=rstd[:], in_=std[:])
+                std[i] = late.tile([P, 1], F32, name="std")
+                nc.scalar.activation(
+                    out=std[i][:], in_=sum_sq[:], func=ACT.Sqrt, bias=eps_col[:], scale=1.0 / D_MODEL
+                )
+                centred[i] = late.tile([P, D_MODEL], F32, name="centred")
+                nc.vector.scalar_tensor_tensor(
+                    out=centred[i][:], in0=r[:], scalar=neg_mean[i][:], in1=gain_bc[:], op0=ALU.add, op1=ALU.mult
+                )
 
-                centred = work.tile([P, D_MODEL], F32, name="centred")
+            def scale_and_store(i):
+                rstd = late.tile([P, 1], F32, name="rstd")
+                nc.vector.reciprocal(out=rstd[:], in_=std[i][:])
+                normed = late.tile([P, D_MODEL], F32, name="normed")
                 nc.vector.scalar_tensor_tensor(
-                    out=centred[:], in0=r[:], scalar=neg_mean[:], in1=gain_bc[:], op0=ALU.add, op1=ALU.mult
+                    out=normed[:], in0=centred[i][:], scalar=rstd[:], in1=shift_bc[:], op0=ALU.mult, op1=ALU.add
                 )
-                normed = work.tile([P, D_MODEL], F32, name="normed")
-                nc.vector.scalar_tensor_tensor(
-                    out=normed[:], in0=centred[:], scalar=rstd[:], in1=shift_bc[:], op0=ALU.mult, op1=ALU.add
-                )
-                nc.sync.dma_start(out=out_rows[toks, :], in_=normed[:])
+                nc.sync.dma_start(out=out_rows[i * P : (i + 1) * P, :], in_=normed[:])
+
+            stages = (
+                (H_REGROUP_STEP, regroup_hidden),
+                (H_QUANTISE_STEP, quantise_hidden),
+                (PRODUCT_STEP, second_product),
+                (CENTRE_STEP, add_and_centre),
+                (STORE_STEP, scale_and_store),
+            )
+            for n in range(H_REGROUP_STEP, LAST_STEP + 1):
+                if n < UNITS:
+                    regroup_unit(n)
+                if n - 1 < UNITS:
+                    quantise_unit(n - 1, w2_codes[:, n - 1 - W1_UNITS, :], w2_scales[:, n - 1 - W1_UNITS, :])
+                for first_step, stage in stages:
+                    if 0 <= n - first_step < TOKEN_TILES:
+                        stage(n - first_step)

@@ -33,9 +33,6 @@ W2_UNITS = PASSES_2
 UNITS = W1_UNITS + W2_UNITS
 RAW_BUFS = 5
 
-SCALAR_COLS = 160
-VECTOR_COLS = UNIT_COLS - SCALAR_COLS
-
 FIRST_PAIR_STEP = 2
 PAIRS_A_STEP = 2
 H_REGROUP_STEP = FIRST_PAIR_STEP + HIDDEN_PAIRS // PAIRS_A_STEP
@@ -110,10 +107,8 @@ def tile_decoderlayer_pb_kernel(tc, h_attn, w1, b1, w2, b2, g2, be2, out):
             raw = raw_units[n]
             grouped = grouped_pool.tile([P, UNIT_COLS, PACK], BF16, name="grouped", align_bytes=64)
             grouped_units[n] = grouped
-            dst, src = regrouped(grouped[:, :VECTOR_COLS, :], raw[:, :, :VECTOR_COLS])
+            dst, src = regrouped(grouped[:], raw[:])
             nc.vector.tensor_copy(out=dst, in_=src)
-            dst, src = regrouped(grouped[:, VECTOR_COLS:, :], raw[:, :, VECTOR_COLS:])
-            nc.scalar.copy(out=dst, in_=src)
             if n + RAW_BUFS < UNITS:
                 load_unit(n + RAW_BUFS)
 
@@ -196,12 +191,13 @@ def tile_decoderlayer_pb_kernel(tc, h_attn, w1, b1, w2, b2, g2, be2, out):
             nc.scalar.dma_start(out=b1_rows[:HIDDEN_TILES, :], in_=b1.rearrange("(f p) -> f p", p=P))
             nc.scalar.dma_start(out=b2_rows[0:1, :], in_=b2.rearrange("(o d) -> o d", o=1))
 
+            load_unit(0)
             for j in range(TOKEN_TILES // 2):
                 nc.sync.dma_start(
                     out=x_sb[:, 2 * j : 2 * j + 2, :],
                     in_=x_rows[j * 2 * P : (j + 1) * 2 * P, :].rearrange("(a p) d -> p a d", p=P),
                 )
-            for n in range(RAW_BUFS):
+            for n in range(1, RAW_BUFS):
                 load_unit(n)
 
             b1_flipped = psum.tile([P, P], BF16, name="b1_flipped", tag="bank")

@@ -192,12 +192,13 @@ def tile_decoderlayer_pb_kernel(tc, h_attn, w1, b1, w2, b2, g2, be2, out):
             nc.scalar.dma_start(out=b2_rows[0:1, :], in_=b2.rearrange("(o d) -> o d", o=1))
 
             load_unit(0)
+            load_unit(1)
             for j in range(TOKEN_TILES // 2):
                 nc.sync.dma_start(
                     out=x_sb[:, 2 * j : 2 * j + 2, :],
                     in_=x_rows[j * 2 * P : (j + 1) * 2 * P, :].rearrange("(a p) d -> p a d", p=P),
                 )
-            for n in range(1, RAW_BUFS):
+            for n in range(2, RAW_BUFS):
                 load_unit(n)
 
             b1_flipped = psum.tile([P, P], BF16, name="b1_flipped", tag="bank")

@@ -28,12 +28,15 @@ PASSES_1 = D_MODEL // K_PASS
 PASSES_2 = D_HIDDEN // K_PASS
 
 UNIT_COLS = 1024
-W1_UNITS = PASSES_1 * (D_HIDDEN // UNIT_COLS)
+W1_COLS = UNIT_COLS // PASSES_1
+W1_UNITS = D_HIDDEN // W1_COLS
 W2_UNITS = PASSES_2
 UNITS = W1_UNITS + W2_UNITS
+EARLY_H = 3
+SCALAR_UNIT = UNITS - 1
 RAW_BUFS = 5
 
-FIRST_PAIR_STEP = 2
+FIRST_PAIR_STEP = 1
 PAIRS_A_STEP = 2
 H_REGROUP_STEP = FIRST_PAIR_STEP + HIDDEN_PAIRS // PAIRS_A_STEP
 H_QUANTISE_STEP = H_REGROUP_STEP + 2
@@ -85,19 +88,23 @@ def tile_decoderlayer_pb_kernel(tc, h_attn, w1, b1, w2, b2, g2, be2, out):
         raw_units = {}
         grouped_units = {}
 
-        def load_unit(n):
-            raw = raw_pool.tile([P, PACK, UNIT_COLS], BF16, name="raw")
-            raw_units[n] = raw
+        def load_unit(n, passes=range(PASSES_1)):
             if n < W1_UNITS:
-                c, g = divmod(n, PASSES_1)
-                cols = slice(c * UNIT_COLS, (c + 1) * UNIT_COLS)
-                for u in range(2):
-                    k0 = g * K_PASS + u * 2 * P
-                    nc.sync.dma_start(
-                        out=raw[:, 2 * u : 2 * u + 2, :],
-                        in_=w1[k0 : k0 + 2 * P, cols].rearrange("(p e) n -> p e n", e=2),
-                    )
+                if n not in raw_units:
+                    raw = raw_pool.tile([P, PASSES_1, PACK, W1_COLS], BF16, name="raw")
+                    raw_units[n] = raw
+                raw = raw_units[n]
+                cols = slice(n * W1_COLS, (n + 1) * W1_COLS)
+                for g in passes:
+                    for u in range(2):
+                        k0 = g * K_PASS + u * 2 * P
+                        nc.sync.dma_start(
+                            out=raw[:, g, 2 * u : 2 * u + 2, :],
+                            in_=w1[k0 : k0 + 2 * P, cols].rearrange("(p e) n -> p e n", e=2),
+                        )
             else:
+                raw = raw_pool.tile([P, PACK, UNIT_COLS], BF16, name="raw")
+                raw_units[n] = raw
                 k0 = (n - W1_UNITS) * K_PASS
                 nc.sync.dma_start(
                     out=raw[:], in_=w2[k0 : k0 + K_PASS, :].rearrange("(t p) n -> p t n", p=P)
@@ -107,8 +114,18 @@ def tile_decoderlayer_pb_kernel(tc, h_attn, w1, b1, w2, b2, g2, be2, out):
             raw = raw_units[n]
             grouped = grouped_pool.tile([P, UNIT_COLS, PACK], BF16, name="grouped", align_bytes=64)
             grouped_units[n] = grouped
-            dst, src = regrouped(grouped[:], raw[:])
-            nc.vector.tensor_copy(out=dst, in_=src)
+            if n == 0:
+                for g in range(PASSES_1):
+                    dst, src = regrouped(grouped[:, g * W1_COLS : (g + 1) * W1_COLS, :], raw[:, g])
+                    nc.vector.tensor_copy(out=dst, in_=src)
+            elif n < W1_UNITS:
+                nc.vector.tensor_copy(
+                    out=grouped[:].rearrange("p (g c i) t -> p g c t i", g=PASSES_1, i=4),
+                    in_=raw[:].rearrange("p g t (c i) -> p g c t i", i=4),
+                )
+            else:
+                dst, src = regrouped(grouped[:], raw[:])
+                nc.vector.tensor_copy(out=dst, in_=src)
             if n + RAW_BUFS < UNITS:
                 load_unit(n + RAW_BUFS)
 
@@ -125,34 +142,36 @@ def tile_decoderlayer_pb_kernel(tc, h_attn, w1, b1, w2, b2, g2, be2, out):
             b1_rows = early.tile([P, P], BF16, name="b1_rows")
             x_codes = early.tile([P, PASSES_1, TOKENS], U32, name="x_codes", align_bytes=64)
             x_scales = early.tile([P, PASSES_1, TOKENS], U8, name="x_scales", align_bytes=64)
-            w1_codes = early.tile([P, PASSES_1, D_HIDDEN], U32, name="w1_codes", align_bytes=64)
-            w1_scales = early.tile([P, PASSES_1, D_HIDDEN], U8, name="w1_scales", align_bytes=64)
-            x_grouped = early.tile([P, PASSES_1, TOKENS, 2], F32, name="x_grouped", align_bytes=64)
+            w1_codes = early.tile([P, W1_UNITS, UNIT_COLS], U32, name="w1_codes", align_bytes=64)
+            w1_scales = early.tile([P, W1_UNITS, UNIT_COLS], U8, name="w1_scales", align_bytes=64)
+            x_grouped = {}
 
             def quantise_w1_unit(n):
-                c, g = divmod(n, PASSES_1)
-                cols = slice(c * UNIT_COLS, (c + 1) * UNIT_COLS)
-                quantise_unit(n, w1_codes[:, g, cols], w1_scales[:, g, cols])
+                quantise_unit(n, w1_codes[:, n, :], w1_scales[:, n, :])
 
             def transpose_tokens(i):
                 words = x_sb[:, i, :].bitcast(F32)
                 flipped = psum.tile([P, 2 * PASSES_1, P], F32, name="flipped", tag="bank")
                 for q in range(2 * PASSES_1):
                     nc.tensor.transpose(flipped[:, q, :], words[:, q * P : (q + 1) * P], ident_f32[:])
+                j, a = divmod(i, 2)
+                if a == 0:
+                    x_grouped[j] = early.tile(
+                        [P, PASSES_1, 2 * P, 2], F32, name="x_grouped", align_bytes=64, bufs=TOKEN_TILES // 2
+                    )
                 nc.scalar.copy(
-                    out=x_grouped[:, :, i * P : (i + 1) * P, :],
+                    out=x_grouped[j][:, :, a * P : (a + 1) * P, :],
                     in_=flipped[:].rearrange("p (g u) w -> p g w u", u=2),
                 )
 
-            def quantise_tokens():
-                for j in range(TOKENS // 256):
-                    toks = slice(j * 256, (j + 1) * 256)
-                    for g in range(PASSES_1):
-                        nc.vector.quantize_mx(
-                            out=x_codes[:, g, toks].bitcast(FP8X4),
-                            scales=x_scales[:, g, toks],
-                            in_=x_grouped[:, g, toks, :].bitcast(BF16).rearrange("p w t -> p (w t)"),
-                        )
+            def quantise_tokens(j):
+                toks = slice(j * 2 * P, (j + 1) * 2 * P)
+                for g in range(PASSES_1):
+                    nc.vector.quantize_mx(
+                        out=x_codes[:, g, toks].bitcast(FP8X4),
+                        scales=x_scales[:, g, toks],
+                        in_=x_grouped[j][:, g].bitcast(BF16).rearrange("p w t -> p (w t)"),
+                    )
 
             def residual_piece(i, half):
                 cols = slice(half * BANK, (half + 1) * BANK)
@@ -170,12 +189,13 @@ def tile_decoderlayer_pb_kernel(tc, h_attn, w1, b1, w2, b2, g2, be2, out):
                     pieces.append((f, main[:], slice(0, BANK)))
                     pieces.append((f, rest[:, a, :], slice(BANK, TOKENS)))
                 for f, acc, toks in pieces:
-                    cols = slice(f * P, (f + 1) * P)
+                    unit, c0 = divmod(f * P, W1_COLS)
                     for g in range(PASSES_1):
+                        cols = slice(g * W1_COLS + c0, g * W1_COLS + c0 + P)
                         nc.tensor.matmul_mx(
                             out=acc,
-                            lhsT=w1_codes[:, g, cols].bitcast(FP8X4),
-                            lhsT_scale=w1_scales[:, g, cols],
+                            lhsT=w1_codes[:, unit, cols].bitcast(FP8X4),
+                            lhsT_scale=w1_scales[:, unit, cols],
                             rhs=x_codes[:, g, toks].bitcast(FP8X4),
                             rhs_scale=x_scales[:, g, toks],
                             start=(g == 0),
@@ -191,36 +211,36 @@ def tile_decoderlayer_pb_kernel(tc, h_attn, w1, b1, w2, b2, g2, be2, out):
             nc.scalar.dma_start(out=b1_rows[:HIDDEN_TILES, :], in_=b1.rearrange("(f p) -> f p", p=P))
             nc.scalar.dma_start(out=b2_rows[0:1, :], in_=b2.rearrange("(o d) -> o d", o=1))
 
-            load_unit(0)
-            load_unit(1)
             for j in range(TOKEN_TILES // 2):
+                if j < PASSES_1:
+                    load_unit(0, (j,))
                 nc.sync.dma_start(
                     out=x_sb[:, 2 * j : 2 * j + 2, :],
                     in_=x_rows[j * 2 * P : (j + 1) * 2 * P, :].rearrange("(a p) d -> p a d", p=P),
                 )
-            for n in range(2, RAW_BUFS):
+            for n in range(1, RAW_BUFS):
                 load_unit(n)
-
-            b1_flipped = psum.tile([P, P], BF16, name="b1_flipped", tag="bank")
-            nc.tensor.transpose(b1_flipped[:], b1_rows[:], ident_bf[:])
-            nc.scalar.copy(out=b1_cols[:], in_=b1_flipped[:])
 
             for i in range(TOKEN_TILES):
                 transpose_tokens(i)
-            regroup_unit(0)
-            quantise_tokens()
-            regroup_unit(1)
-            quantise_w1_unit(0)
+            with tc.manual_schedule(engines={mybir.EngineType.DVE}):
+                regroup_unit(0)
+                quantise_tokens(0)
+                quantise_w1_unit(0)
+                quantise_tokens(1)
+                quantise_tokens(2)
+                regroup_unit(1)
+            b1_flipped = psum.tile([P, P], BF16, name="b1_flipped", tag="bank")
+            nc.tensor.transpose(b1_flipped[:], b1_rows[:], ident_bf[:])
+            nc.scalar.copy(out=b1_cols[:], in_=b1_flipped[:])
             for i in range(TOKEN_TILES):
                 for half in range(2):
                     residual_piece(i, half)
 
             for n in range(FIRST_PAIR_STEP, H_REGROUP_STEP):
-                regroup_unit(n)
-                if n - 1 < W1_UNITS:
+                if n > 1:
+                    regroup_unit(n)
                     quantise_w1_unit(n - 1)
-                else:
-                    quantise_unit(n - 1, w2_codes[:, n - 1 - W1_UNITS, :], w2_scales[:, n - 1 - W1_UNITS, :])
                 for q in range(PAIRS_A_STEP * (n - FIRST_PAIR_STEP), PAIRS_A_STEP * (n - FIRST_PAIR_STEP + 1)):
                     hidden_pair(q)
 
@@ -293,7 +313,7 @@ def tile_decoderlayer_pb_kernel(tc, h_attn, w1, b1, w2, b2, g2, be2, out):
                     op0=ALU.add,
                     op1=ALU.mult,
                 )
-                squares = late.tile([P, D_MODEL], BF16, name="squares")
+                squares = late.tile([P, D_MODEL], BF16, name="squares", bufs=1)
                 sum_sq = late.tile([P, 1], F32, name="sum_sq")
                 nc.scalar.activation(
                     out=squares[:], in_=r[:], func=ACT.Square, bias=neg_mean[i][:], scale=1.0, accum_out=sum_sq[:]
@@ -302,7 +322,7 @@ def tile_decoderlayer_pb_kernel(tc, h_attn, w1, b1, w2, b2, g2, be2, out):
                 nc.scalar.activation(
                     out=std[i][:], in_=sum_sq[:], func=ACT.Sqrt, bias=eps_col[:], scale=1.0 / D_MODEL
                 )
-                centred[i] = late.tile([P, D_MODEL], F32, name="centred")
+                centred[i] = late.tile([P, D_MODEL], F32, name="centred", bufs=2)
                 nc.vector.scalar_tensor_tensor(
                     out=centred[i][:], in0=r[:], scalar=neg_mean[i][:], in1=gain_bc[:], op0=ALU.add, op1=ALU.mult
                 )
@@ -316,18 +336,28 @@ def tile_decoderlayer_pb_kernel(tc, h_attn, w1, b1, w2, b2, g2, be2, out):
                 )
                 nc.sync.dma_start(out=out_rows[i * P : (i + 1) * P, :], in_=normed[:])
 
+            def early_then_late(first, count, then):
+                return [first + i if i < count else then + i - count for i in range(TOKEN_TILES)]
+
             stages = (
-                (H_REGROUP_STEP, regroup_hidden),
-                (H_QUANTISE_STEP, quantise_hidden),
-                (PRODUCT_STEP, second_product),
-                (CENTRE_STEP, add_and_centre),
-                (STORE_STEP, scale_and_store),
+                (early_then_late(H_REGROUP_STEP, EARLY_H, PRODUCT_STEP + EARLY_H - 1), regroup_hidden),
+                (early_then_late(H_QUANTISE_STEP, EARLY_H, PRODUCT_STEP + EARLY_H), quantise_hidden),
+                (early_then_late(PRODUCT_STEP, TOKEN_TILES, 0), second_product),
+                (early_then_late(CENTRE_STEP, TOKEN_TILES, 0), add_and_centre),
+                (early_then_late(STORE_STEP, TOKEN_TILES, 0), scale_and_store),
             )
+            scalar_grouped = late.tile([P, UNIT_COLS, PACK], BF16, name="scalar_grouped", align_bytes=64, bufs=1)
+            grouped_units[SCALAR_UNIT] = scalar_grouped
             for n in range(H_REGROUP_STEP, LAST_STEP + 1):
-                if n < UNITS:
+                if n < SCALAR_UNIT:
                     regroup_unit(n)
                 if n - 1 < UNITS:
                     quantise_unit(n - 1, w2_codes[:, n - 1 - W1_UNITS, :], w2_scales[:, n - 1 - W1_UNITS, :])
-                for first_step, stage in stages:
-                    if 0 <= n - first_step < TOKEN_TILES:
-                        stage(n - first_step)
+                for steps, stage in stages:
+                    if n in steps:
+                        stage(steps.index(n))
+                if n == H_REGROUP_STEP:
+                    for half in range(2):
+                        cols = slice(half * BANK, (half + 1) * BANK)
+                        dst, src = regrouped(scalar_grouped[:, cols, :], raw_units[SCALAR_UNIT][:, :, cols])
+                        nc.scalar.copy(out=dst, in_=src)

@@ -83,7 +83,7 @@ def tile_decoderlayer_pb_kernel(tc, h_attn, w1, b1, w2, b2, g2, be2, out):
         nc.vector.memset(ones_bf[:], 1.0)
         nc.vector.memset(eps_col[:], EPS)
         warm = keep.tile([P, 1], F32, name="warm")
-        nc.scalar.activation(out=warm[:], in_=eps_col[:], func=ACT.Sqrt)
+        nc.scalar.activation(out=warm[:], in_=eps_col[:], func=ACT.Abs_reciprocal_sqrt)
 
         raw_units = {}
         grouped_units = {}
@@ -253,7 +253,8 @@ def tile_decoderlayer_pb_kernel(tc, h_attn, w1, b1, w2, b2, g2, be2, out):
             h_scales = {}
             ffn = {}
             neg_mean = {}
-            std = {}
+            rstd = {}
+            rows = {}
             centred = {}
 
             def regroup_hidden(i):
@@ -290,7 +291,7 @@ def tile_decoderlayer_pb_kernel(tc, h_attn, w1, b1, w2, b2, g2, be2, out):
                             stop=(g == PASSES_2 - 1),
                         )
 
-            def add_and_centre(i):
+            def add_residual(i):
                 r = late.tile([P, D_MODEL], F32, name="r")
                 row_sum = late.tile([P, 2], F32, name="row_sum")
                 for half in range(2):
@@ -305,34 +306,31 @@ def tile_decoderlayer_pb_kernel(tc, h_attn, w1, b1, w2, b2, g2, be2, out):
                         accum_out=row_sum[:, half : half + 1],
                     )
                 neg_mean[i] = late.tile([P, 1], F32, name="neg_mean")
-                nc.vector.tensor_scalar(
-                    out=neg_mean[i][:],
-                    in0=row_sum[:, 0:1],
-                    scalar1=row_sum[:, 1:2],
-                    scalar2=-1.0 / D_MODEL,
-                    op0=ALU.add,
-                    op1=ALU.mult,
+                scaled_sums = late.tile([P, 2], F32, name="scaled_sums")
+                nc.scalar.activation(
+                    out=scaled_sums[:], in_=row_sum[:], func=ACT.Copy, scale=-1.0 / D_MODEL, accum_out=neg_mean[i][:]
                 )
                 squares = late.tile([P, D_MODEL], BF16, name="squares", bufs=1)
                 sum_sq = late.tile([P, 1], F32, name="sum_sq")
                 nc.scalar.activation(
                     out=squares[:], in_=r[:], func=ACT.Square, bias=neg_mean[i][:], scale=1.0, accum_out=sum_sq[:]
                 )
-                std[i] = late.tile([P, 1], F32, name="std")
+                rstd[i] = late.tile([P, 1], F32, name="rstd")
                 nc.scalar.activation(
-                    out=std[i][:], in_=sum_sq[:], func=ACT.Sqrt, bias=eps_col[:], scale=1.0 / D_MODEL
+                    out=rstd[i][:], in_=sum_sq[:], func=ACT.Abs_reciprocal_sqrt, bias=eps_col[:], scale=1.0 / D_MODEL
                 )
+                rows[i] = r
+
+            def centre(i):
                 centred[i] = late.tile([P, D_MODEL], F32, name="centred", bufs=2)
                 nc.vector.scalar_tensor_tensor(
-                    out=centred[i][:], in0=r[:], scalar=neg_mean[i][:], in1=gain_bc[:], op0=ALU.add, op1=ALU.mult
+                    out=centred[i][:], in0=rows[i][:], scalar=neg_mean[i][:], in1=gain_bc[:], op0=ALU.add, op1=ALU.mult
                 )
 
             def scale_and_store(i):
-                rstd = late.tile([P, 1], F32, name="rstd")
-                nc.vector.reciprocal(out=rstd[:], in_=std[i][:])
                 normed = late.tile([P, D_MODEL], F32, name="normed")
                 nc.vector.scalar_tensor_tensor(
-                    out=normed[:], in0=centred[i][:], scalar=rstd[:], in1=shift_bc[:], op0=ALU.mult, op1=ALU.add
+                    out=normed[:], in0=centred[i][:], scalar=rstd[i][:], in1=shift_bc[:], op0=ALU.mult, op1=ALU.add
                 )
                 nc.sync.dma_start(out=out_rows[i * P : (i + 1) * P, :], in_=normed[:])
 
@@ -343,8 +341,9 @@ def tile_decoderlayer_pb_kernel(tc, h_attn, w1, b1, w2, b2, g2, be2, out):
                 (early_then_late(H_REGROUP_STEP, EARLY_H, PRODUCT_STEP + EARLY_H - 1), regroup_hidden),
                 (early_then_late(H_QUANTISE_STEP, EARLY_H, PRODUCT_STEP + EARLY_H), quantise_hidden),
                 (early_then_late(PRODUCT_STEP, TOKEN_TILES, 0), second_product),
-                (early_then_late(CENTRE_STEP, TOKEN_TILES, 0), add_and_centre),
+                (early_then_late(CENTRE_STEP, TOKEN_TILES, 0), add_residual),
                 (early_then_late(STORE_STEP, TOKEN_TILES, 0), scale_and_store),
+                (early_then_late(CENTRE_STEP, TOKEN_TILES, 0), centre),
             )
             scalar_grouped = late.tile([P, UNIT_COLS, PACK], BF16, name="scalar_grouped", align_bytes=64, bufs=1)
             grouped_units[SCALAR_UNIT] = scalar_grouped

@@ -110,15 +110,22 @@ def tile_decoderlayer_pb_kernel(tc, h_attn, w1, b1, w2, b2, g2, be2, out):
                     out=raw[:], in_=w2[k0 : k0 + K_PASS, :].rearrange("(t p) n -> p t n", p=P)
                 )
 
+        def regroup_pass(n, g):
+            if g == 0:
+                grouped = grouped_pool.tile([P, UNIT_COLS, PACK], BF16, name="grouped", align_bytes=64)
+                grouped_units[n] = grouped
+            dst, src = regrouped(
+                grouped_units[n][:, g * W1_COLS : (g + 1) * W1_COLS, :], raw_units[n][:, g]
+            )
+            nc.vector.tensor_copy(out=dst, in_=src)
+            if g == PASSES_1 - 1:
+                load_unit(n + RAW_BUFS)
+
         def regroup_unit(n):
             raw = raw_units[n]
             grouped = grouped_pool.tile([P, UNIT_COLS, PACK], BF16, name="grouped", align_bytes=64)
             grouped_units[n] = grouped
-            if n == 0:
-                for g in range(PASSES_1):
-                    dst, src = regrouped(grouped[:, g * W1_COLS : (g + 1) * W1_COLS, :], raw[:, g])
-                    nc.vector.tensor_copy(out=dst, in_=src)
-            elif n < W1_UNITS:
+            if n < W1_UNITS:
                 nc.vector.tensor_copy(
                     out=grouped[:].rearrange("p (g c i) t -> p g c t i", g=PASSES_1, i=4),
                     in_=raw[:].rearrange("p g t (c i) -> p g c t i", i=4),
@@ -173,12 +180,13 @@ def tile_decoderlayer_pb_kernel(tc, h_attn, w1, b1, w2, b2, g2, be2, out):
                         in_=x_grouped[j][:, g].bitcast(BF16).rearrange("p w t -> p (w t)"),
                     )
 
-            def residual_piece(i, half):
-                cols = slice(half * BANK, (half + 1) * BANK)
-                acc = psum.tile([P, BANK], F32, name="resid_acc", tag="bank")
-                nc.tensor.matmul(out=acc[:], lhsT=ident_bf[:], rhs=x_sb[:, i, cols], start=True, stop=False)
-                nc.tensor.matmul(out=acc[:], lhsT=ones_bf[:], rhs=b2_rows[:, cols], start=False, stop=True)
-                nc.scalar.copy(out=resid[:, i, cols], in_=acc[:])
+            def residual(i):
+                for half in range(2):
+                    cols = slice(half * BANK, (half + 1) * BANK)
+                    acc = psum.tile([P, BANK], F32, name="resid_acc", tag="bank")
+                    nc.tensor.matmul(out=acc[:], lhsT=ident_bf[:], rhs=x_sb[:, i, cols], start=True, stop=False)
+                    nc.tensor.matmul(out=acc[:], lhsT=ones_bf[:], rhs=b2_rows[:, cols], start=False, stop=True)
+                    nc.scalar.copy(out=resid[:, i, cols], in_=acc[:])
 
             def hidden_pair(q):
                 rest = psum.tile([P, 2, TOKENS - BANK], F32, name="rest", tag="bank")
@@ -211,31 +219,33 @@ def tile_decoderlayer_pb_kernel(tc, h_attn, w1, b1, w2, b2, g2, be2, out):
             nc.scalar.dma_start(out=b1_rows[:HIDDEN_TILES, :], in_=b1.rearrange("(f p) -> f p", p=P))
             nc.scalar.dma_start(out=b2_rows[0:1, :], in_=b2.rearrange("(o d) -> o d", o=1))
 
+            load_unit(0, (0,))
             for j in range(TOKEN_TILES // 2):
-                if j < PASSES_1:
-                    load_unit(0, (j,))
                 nc.sync.dma_start(
                     out=x_sb[:, 2 * j : 2 * j + 2, :],
                     in_=x_rows[j * 2 * P : (j + 1) * 2 * P, :].rearrange("(a p) d -> p a d", p=P),
                 )
-            for n in range(1, RAW_BUFS):
+                unit, g = divmod(j + 1, PASSES_1)
+                load_unit(unit, (g,))
+            for n in range(2, RAW_BUFS):
                 load_unit(n)
 
-            for i in range(TOKEN_TILES):
-                transpose_tokens(i)
-            with tc.manual_schedule(engines={mybir.EngineType.DVE}):
-                regroup_unit(0)
-                quantise_tokens(0)
-                quantise_w1_unit(0)
-                quantise_tokens(1)
-                quantise_tokens(2)
-                regroup_unit(1)
-            b1_flipped = psum.tile([P, P], BF16, name="b1_flipped", tag="bank")
-            nc.tensor.transpose(b1_flipped[:], b1_rows[:], ident_bf[:])
-            nc.scalar.copy(out=b1_cols[:], in_=b1_flipped[:])
-            for i in range(TOKEN_TILES):
-                for half in range(2):
-                    residual_piece(i, half)
+            with tc.manual_schedule(engines={mybir.EngineType.DVE, mybir.EngineType.PE, mybir.EngineType.Activation}):
+                regroup_pass(0, 0)
+                for j in range(TOKEN_TILES // 2):
+                    transpose_tokens(2 * j)
+                    transpose_tokens(2 * j + 1)
+                    residual(j)
+                    unit, g = divmod(j + 1, PASSES_1)
+                    regroup_pass(unit, g)
+                    quantise_tokens(j)
+                    if j == 0:
+                        quantise_w1_unit(0)
+                b1_flipped = psum.tile([P, P], BF16, name="b1_flipped", tag="bank")
+                nc.tensor.transpose(b1_flipped[:], b1_rows[:], ident_bf[:])
+                nc.scalar.copy(out=b1_cols[:], in_=b1_flipped[:])
+                for i in range(TOKEN_TILES // 2, TOKEN_TILES):
+                    residual(i)
 
             for n in range(FIRST_PAIR_STEP, H_REGROUP_STEP):
                 if n > 1:
@@ -329,10 +339,18 @@ def tile_decoderlayer_pb_kernel(tc, h_attn, w1, b1, w2, b2, g2, be2, out):
 
             def scale_and_store(i):
                 normed = late.tile([P, D_MODEL], F32, name="normed")
-                nc.vector.scalar_tensor_tensor(
-                    out=normed[:], in0=centred[i][:], scalar=rstd[i][:], in1=shift_bc[:], op0=ALU.mult, op1=ALU.add
-                )
-                nc.sync.dma_start(out=out_rows[i * P : (i + 1) * P, :], in_=normed[:])
+                width = D_MODEL // 2 if i == TOKEN_TILES - 1 else D_MODEL
+                for d0 in range(0, D_MODEL, width):
+                    cols = slice(d0, d0 + width)
+                    nc.vector.scalar_tensor_tensor(
+                        out=normed[:, cols],
+                        in0=centred[i][:, cols],
+                        scalar=rstd[i][:],
+                        in1=shift_bc[:, cols],
+                        op0=ALU.mult,
+                        op1=ALU.add,
+                    )
+                    nc.sync.dma_start(out=out_rows[i * P : (i + 1) * P, cols], in_=normed[:, cols])
 
             def early_then_late(first, count, then):
                 return [first + i if i < count else then + i - count for i in range(TOKEN_TILES)]

@@ -33,6 +33,7 @@ W1_UNITS = D_HIDDEN // W1_COLS
 W2_UNITS = PASSES_2
 UNITS = W1_UNITS + W2_UNITS
 EARLY_H = 3
+SCALAR_RUN = 2
 SCALAR_UNIT = UNITS - 1
 RAW_BUFS = 5
 
@@ -48,10 +49,10 @@ LAST_STEP = STORE_STEP + TOKEN_TILES - 1
 FLOPS = 2 * 2 * TOKENS * D_MODEL * D_HIDDEN
 
 
-def regrouped(dst, src):
+def regrouped(dst, src, run=4):
     return (
-        dst.rearrange("p (c i) t -> p c t i", i=4),
-        src.rearrange("p t (c i) -> p c t i", i=4),
+        dst.rearrange("p (c i) t -> p c t i", i=run),
+        src.rearrange("p t (c i) -> p c t i", i=run),
     )
 
 
@@ -271,7 +272,7 @@ def tile_decoderlayer_pb_kernel(tc, h_attn, w1, b1, w2, b2, g2, be2, out):
                 toks = slice(i * P, (i + 1) * P)
                 h_grouped[i] = late.tile([P, PASSES_2, P, PACK], BF16, name="h_grouped", align_bytes=64)
                 for g in range(PASSES_2):
-                    dst, src = regrouped(h_grouped[i][:, g], hidden[:, PACK * g : PACK * (g + 1), toks])
+                    dst, src = regrouped(h_grouped[i][:, g], hidden[:, PACK * g : PACK * (g + 1), toks], SCALAR_RUN)
                     nc.scalar.copy(out=dst, in_=src)
 
             def quantise_hidden(i):
@@ -376,5 +377,5 @@ def tile_decoderlayer_pb_kernel(tc, h_attn, w1, b1, w2, b2, g2, be2, out):
                 if n == H_REGROUP_STEP:
                     for half in range(2):
                         cols = slice(half * BANK, (half + 1) * BANK)
-                        dst, src = regrouped(scalar_grouped[:, cols, :], raw_units[SCALAR_UNIT][:, :, cols])
+                        dst, src = regrouped(scalar_grouped[:, cols, :], raw_units[SCALAR_UNIT][:, :, cols], SCALAR_RUN)
                         nc.scalar.copy(out=dst, in_=src)

@@ -33,6 +33,7 @@ W1_UNITS = D_HIDDEN // W1_COLS
 W2_UNITS = PASSES_2
 UNITS = W1_UNITS + W2_UNITS
 EARLY_H = 3
+HEAD_RESIDUALS = 3
 SCALAR_RUN = 2
 SCALAR_UNIT = UNITS - 1
 RAW_BUFS = 5
@@ -79,6 +80,8 @@ def tile_decoderlayer_pb_kernel(tc, h_attn, w1, b1, w2, b2, g2, be2, out):
         gain_bc = keep.tile([P, D_MODEL], BF16, name="gain_bc")
         shift_bc = keep.tile([P, D_MODEL], BF16, name="shift_bc")
 
+        b2_rows = keep.tile([P, D_MODEL], BF16, name="b2_rows")
+        nc.vector.memset(b2_rows[:].bitcast(F32), 0.0)
         make_identity(nc, ident_f32[:])
         make_identity(nc, ident_bf[:])
         nc.vector.memset(ones_bf[:], 1.0)
@@ -146,7 +149,6 @@ def tile_decoderlayer_pb_kernel(tc, h_attn, w1, b1, w2, b2, g2, be2, out):
 
         with tc.tile_pool(name="early", bufs=1) as early:
             x_sb = early.tile([P, TOKEN_TILES, D_MODEL], BF16, name="x_sb")
-            b2_rows = early.tile([P, D_MODEL], BF16, name="b2_rows")
             b1_rows = early.tile([P, P], BF16, name="b1_rows")
             x_codes = early.tile([P, PASSES_1, TOKENS], U32, name="x_codes", align_bytes=64)
             x_scales = early.tile([P, PASSES_1, TOKENS], U8, name="x_scales", align_bytes=64)
@@ -216,44 +218,49 @@ def tile_decoderlayer_pb_kernel(tc, h_attn, w1, b1, w2, b2, g2, be2, out):
                     )
 
             nc.vector.memset(b1_rows[:], 0.0)
-            nc.vector.memset(b2_rows[:], 0.0)
             nc.scalar.dma_start(out=b1_rows[:HIDDEN_TILES, :], in_=b1.rearrange("(f p) -> f p", p=P))
-            nc.scalar.dma_start(out=b2_rows[0:1, :], in_=b2.rearrange("(o d) -> o d", o=1))
 
+            def load_tokens(i):
+                nc.sync.dma_start(out=x_sb[:, i, :], in_=x_rows[i * P : (i + 1) * P, :])
+
+            load_tokens(0)
             load_unit(0, (0,))
-            for j in range(TOKEN_TILES // 2):
-                nc.sync.dma_start(
-                    out=x_sb[:, 2 * j : 2 * j + 2, :],
-                    in_=x_rows[j * 2 * P : (j + 1) * 2 * P, :].rearrange("(a p) d -> p a d", p=P),
-                )
-                unit, g = divmod(j + 1, PASSES_1)
-                load_unit(unit, (g,))
+            nc.sync.dma_start(out=b2_rows[0:1, :], in_=b2.rearrange("(o d) -> o d", o=1))
+            load_unit(0, (1,))
+            for i in range(1, TOKEN_TILES):
+                load_tokens(i)
+                if i <= PASSES_1:
+                    load_unit(1, (i - 1,))
             for n in range(2, RAW_BUFS):
                 load_unit(n)
 
             with tc.manual_schedule(engines={mybir.EngineType.DVE, mybir.EngineType.PE, mybir.EngineType.Activation}):
-                regroup_pass(0, 0)
-                for j in range(TOKEN_TILES // 2):
-                    transpose_tokens(2 * j)
-                    transpose_tokens(2 * j + 1)
-                    residual(j)
-                    unit, g = divmod(j + 1, PASSES_1)
-                    regroup_pass(unit, g)
-                    quantise_tokens(j)
-                    if j == 0:
-                        quantise_w1_unit(0)
+                for g in range(PASSES_1):
+                    regroup_pass(0, g)
+                for i in range(TOKEN_TILES):
+                    transpose_tokens(i)
+                    if i < HEAD_RESIDUALS:
+                        residual(i)
+                    j, a = divmod(i, 2)
+                    if a == 1:
+                        if j == 0:
+                            quantise_w1_unit(0)
+                        if j == 1:
+                            for g in range(PASSES_1):
+                                regroup_pass(1, g)
+                        quantise_tokens(j)
                 b1_flipped = psum.tile([P, P], BF16, name="b1_flipped", tag="bank")
                 nc.tensor.transpose(b1_flipped[:], b1_rows[:], ident_bf[:])
                 nc.scalar.copy(out=b1_cols[:], in_=b1_flipped[:])
-                for i in range(TOKEN_TILES // 2, TOKEN_TILES):
+                for i in range(HEAD_RESIDUALS, TOKEN_TILES):
                     residual(i)
 
-            for n in range(FIRST_PAIR_STEP, H_REGROUP_STEP):
-                if n > 1:
-                    regroup_unit(n)
-                    quantise_w1_unit(n - 1)
-                for q in range(PAIRS_A_STEP * (n - FIRST_PAIR_STEP), PAIRS_A_STEP * (n - FIRST_PAIR_STEP + 1)):
-                    hidden_pair(q)
+                for n in range(FIRST_PAIR_STEP, H_REGROUP_STEP):
+                    if n > 1:
+                        regroup_unit(n)
+                        quantise_w1_unit(n - 1)
+                    for q in range(PAIRS_A_STEP * (n - FIRST_PAIR_STEP), PAIRS_A_STEP * (n - FIRST_PAIR_STEP + 1)):
+                        hidden_pair(q)
 
         with tc.tile_pool(name="late", bufs=3, reuse_waits="tile") as late:
             nc.sync.dma_start(out=gain_bc[:], in_=g2.partition_broadcast(P))

from contextlib import ExitStack

import concourse.mybir as mybir
from concourse.masks import make_identity

F32 = mybir.dt.float32
BF16 = mybir.dt.bfloat16
U32 = mybir.dt.uint32
U8 = mybir.dt.uint8
FP8X4 = mybir.dt.float8_e4m3fn_x4
ALU = mybir.AluOpType
ACT = mybir.ActivationFunctionType

P = 128
PACK = 4
K_PASS = P * PACK
BANK = 512

TOKENS = 768
D_MODEL = 1024
D_HIDDEN = 3072
EPS = 1e-6

TOKEN_TILES = TOKENS // P
HIDDEN_TILES = D_HIDDEN // P
HIDDEN_PAIRS = HIDDEN_TILES // 2
PASSES_1 = D_MODEL // K_PASS
PASSES_2 = D_HIDDEN // K_PASS

UNIT_COLS = 1024
W1_COLS = UNIT_COLS // PASSES_1
W1_UNITS = D_HIDDEN // W1_COLS
W2_UNITS = PASSES_2
UNITS = W1_UNITS + W2_UNITS
EARLY_H = 3
HEAD_RESIDUALS = 3
SCALAR_RUN = 2
SCALAR_UNIT = UNITS - 1
RAW_BUFS = 5

FIRST_PAIR_STEP = 1
PAIRS_A_STEP = 2
H_REGROUP_STEP = FIRST_PAIR_STEP + HIDDEN_PAIRS // PAIRS_A_STEP
H_QUANTISE_STEP = H_REGROUP_STEP + 2
PRODUCT_STEP = UNITS
CENTRE_STEP = PRODUCT_STEP + 1
STORE_STEP = CENTRE_STEP + 1
LAST_STEP = STORE_STEP + TOKEN_TILES - 1

FLOPS = 2 * 2 * TOKENS * D_MODEL * D_HIDDEN


def regrouped(dst, src, run=4):
    return (
        dst.rearrange("p (c i) t -> p c t i", i=run),
        src.rearrange("p t (c i) -> p c t i", i=run),
    )


def tile_decoderlayer_pb_kernel(tc, h_attn, w1, b1, w2, b2, g2, be2, out):
    nc = tc.nc
    x_rows = h_attn.flatten_outer_dims()
    out_rows = out.flatten_outer_dims()

    with ExitStack() as whole:
        keep = whole.enter_context(tc.tile_pool(name="keep", bufs=1))
        raw_pool = whole.enter_context(tc.tile_pool(name="raw", bufs=RAW_BUFS))
        grouped_pool = whole.enter_context(tc.tile_pool(name="grouped", bufs=3))
        psum = whole.enter_context(tc.psum_pool(name="psum", bufs=8))

        ident_f32 = keep.tile([P, P], F32, name="ident_f32")
        ident_bf = keep.tile([P, P], BF16, name="ident_bf")
        ones_bf = keep.tile([P, P], BF16, name="ones_bf")
        eps_col = keep.tile([P, 1], F32, name="eps_col")
        b1_cols = keep.tile([P, P], F32, name="b1_cols")
        w2_codes = keep.tile([P, PASSES_2, D_MODEL], U32, name="w2_codes", align_bytes=64)
        w2_scales = keep.tile([P, PASSES_2, D_MODEL], U8, name="w2_scales", align_bytes=64)
        hidden = keep.tile([P, HIDDEN_TILES, TOKENS], BF16, name="hidden")
        resid = keep.tile([P, TOKEN_TILES, D_MODEL], F32, name="resid")
        gain_bc = keep.tile([P, D_MODEL], BF16, name="gain_bc")
        shift_bc = keep.tile([P, D_MODEL], BF16, name="shift_bc")

        b2_rows = keep.tile([P, D_MODEL], BF16, name="b2_rows")
        nc.vector.memset(b2_rows[:].bitcast(F32), 0.0)
        make_identity(nc, ident_f32[:])
        make_identity(nc, ident_bf[:])
        nc.vector.memset(ones_bf[:], 1.0)
        nc.vector.memset(eps_col[:], EPS)
        warm = keep.tile([P, 1], F32, name="warm")
        nc.scalar.activation(out=warm[:], in_=eps_col[:], func=ACT.Abs_reciprocal_sqrt)

        raw_units = {}
        grouped_units = {}

        def load_unit(n, passes=range(PASSES_1)):
            if n < W1_UNITS:
                if n not in raw_units:
                    raw = raw_pool.tile([P, PASSES_1, PACK, W1_COLS], BF16, name="raw")
                    raw_units[n] = raw
                raw = raw_units[n]
                cols = slice(n * W1_COLS, (n + 1) * W1_COLS)
                for g in passes:
                    for u in range(2):
                        k0 = g * K_PASS + u * 2 * P
                        nc.sync.dma_start(
                            out=raw[:, g, 2 * u : 2 * u + 2, :],
                            in_=w1[k0 : k0 + 2 * P, cols].rearrange("(p e) n -> p e n", e=2),
                        )
            else:
                raw = raw_pool.tile([P, PACK, UNIT_COLS], BF16, name="raw")
                raw_units[n] = raw
                k0 = (n - W1_UNITS) * K_PASS
                nc.sync.dma_start(
                    out=raw[:], in_=w2[k0 : k0 + K_PASS, :].rearrange("(t p) n -> p t n", p=P)
                )

        def regroup_pass(n, g):
            if g == 0:
                grouped = grouped_pool.tile([P, UNIT_COLS, PACK], BF16, name="grouped", align_bytes=64)
                grouped_units[n] = grouped
            dst, src = regrouped(
                grouped_units[n][:, g * W1_COLS : (g + 1) * W1_COLS, :], raw_units[n][:, g]
            )
            nc.vector.tensor_copy(out=dst, in_=src)
            if g == PASSES_1 - 1:
                load_unit(n + RAW_BUFS)

        def regroup_unit(n):
            raw = raw_units[n]
            grouped = grouped_pool.tile([P, UNIT_COLS, PACK], BF16, name="grouped", align_bytes=64)
            grouped_units[n] = grouped
            if n < W1_UNITS:
                nc.vector.tensor_copy(
                    out=grouped[:].rearrange("p (g c i) t -> p g c t i", g=PASSES_1, i=4),
                    in_=raw[:].rearrange("p g t (c i) -> p g c t i", i=4),
                )
            else:
                dst, src = regrouped(grouped[:], raw[:])
                nc.vector.tensor_copy(out=dst, in_=src)
            if n + RAW_BUFS < UNITS:
                load_unit(n + RAW_BUFS)

        def quantise_unit(n, codes, scales):
            nc.vector.quantize_mx(
                out=codes.bitcast(FP8X4),
                scales=scales,
                in_=grouped_units[n][:].rearrange("p w t -> p (w t)"),
            )

        with tc.tile_pool(name="early", bufs=1) as early:
            x_sb = early.tile([P, TOKEN_TILES, D_MODEL], BF16, name="x_sb")
            b1_rows = early.tile([P, P], BF16, name="b1_rows")
            x_codes = early.tile([P, PASSES_1, TOKENS], U32, name="x_codes", align_bytes=64)
            x_scales = early.tile([P, PASSES_1, TOKENS], U8, name="x_scales", align_bytes=64)
            w1_codes = early.tile([P, W1_UNITS, UNIT_COLS], U32, name="w1_codes", align_bytes=64)
            w1_scales = early.tile([P, W1_UNITS, UNIT_COLS], U8, name="w1_scales", align_bytes=64)
            x_grouped = {}

            def quantise_w1_unit(n):
                quantise_unit(n, w1_codes[:, n, :], w1_scales[:, n, :])

            def transpose_tokens(i):
                words = x_sb[:, i, :].bitcast(F32)
                flipped = psum.tile([P, 2 * PASSES_1, P], F32, name="flipped", tag="bank")
                for q in range(2 * PASSES_1):
                    nc.tensor.transpose(flipped[:, q, :], words[:, q * P : (q + 1) * P], ident_f32[:])
                j, a = divmod(i, 2)
                if a == 0:
                    x_grouped[j] = early.tile(
                        [P, PASSES_1, 2 * P, 2], F32, name="x_grouped", align_bytes=64, bufs=TOKEN_TILES // 2
                    )
                nc.scalar.copy(
                    out=x_grouped[j][:, :, a * P : (a + 1) * P, :],
                    in_=flipped[:].rearrange("p (g u) w -> p g w u", u=2),
                )

            def quantise_tokens(j):
                toks = slice(j * 2 * P, (j + 1) * 2 * P)
                for g in range(PASSES_1):
                    nc.vector.quantize_mx(
                        out=x_codes[:, g, toks].bitcast(FP8X4),
                        scales=x_scales[:, g, toks],
                        in_=x_grouped[j][:, g].bitcast(BF16).rearrange("p w t -> p (w t)"),
                    )

            def residual(i):
                for half in range(2):
                    cols = slice(half * BANK, (half + 1) * BANK)
                    acc = psum.tile([P, BANK], F32, name="resid_acc", tag="bank")
                    nc.tensor.matmul(out=acc[:], lhsT=ident_bf[:], rhs=x_sb[:, i, cols], start=True, stop=False)
                    nc.tensor.matmul(out=acc[:], lhsT=ones_bf[:], rhs=b2_rows[:, cols], start=False, stop=True)
                    nc.scalar.copy(out=resid[:, i, cols], in_=acc[:])

            def hidden_pair(q):
                rest = psum.tile([P, 2, TOKENS - BANK], F32, name="rest", tag="bank")
                pieces = []
                for a in range(2):
                    f = 2 * q + a
                    main = psum.tile([P, BANK], F32, name="main", tag="bank")
                    pieces.append((f, main[:], slice(0, BANK)))
                    pieces.append((f, rest[:, a, :], slice(BANK, TOKENS)))
                for f, acc, toks in pieces:
                    unit, c0 = divmod(f * P, W1_COLS)
                    for g in range(PASSES_1):
                        cols = slice(g * W1_COLS + c0, g * W1_COLS + c0 + P)
                        nc.tensor.matmul_mx(
                            out=acc,
                            lhsT=w1_codes[:, unit, cols].bitcast(FP8X4),
                            lhsT_scale=w1_scales[:, unit, cols],
                            rhs=x_codes[:, g, toks].bitcast(FP8X4),
                            rhs_scale=x_scales[:, g, toks],
                            start=(g == 0),
                            stop=(g == PASSES_1 - 1),
                        )
                for f, acc, toks in pieces:
                    nc.scalar.activation(
                        out=hidden[:, f, toks], in_=acc, func=ACT.Relu, bias=b1_cols[:, f : f + 1], scale=1.0
                    )

            nc.vector.memset(b1_rows[:], 0.0)
            nc.scalar.dma_start(out=b1_rows[:HIDDEN_TILES, :], in_=b1.rearrange("(f p) -> f p", p=P))

            def load_tokens(i):
                nc.sync.dma_start(out=x_sb[:, i, :], in_=x_rows[i * P : (i + 1) * P, :])

            load_tokens(0)
            load_unit(0, (0,))
            nc.sync.dma_start(out=b2_rows[0:1, :], in_=b2.rearrange("(o d) -> o d", o=1))
            load_unit(0, (1,))
            for i in range(1, TOKEN_TILES):
                load_tokens(i)
                if i <= PASSES_1:
                    load_unit(1, (i - 1,))
            for n in range(2, RAW_BUFS):
                load_unit(n)

            with tc.manual_schedule(engines={mybir.EngineType.DVE, mybir.EngineType.PE, mybir.EngineType.Activation}):
                for g in range(PASSES_1):
                    regroup_pass(0, g)
                for i in range(TOKEN_TILES):
                    transpose_tokens(i)
                    if i < HEAD_RESIDUALS:
                        residual(i)
                    j, a = divmod(i, 2)
                    if a == 1:
                        if j == 0:
                            quantise_w1_unit(0)
                        if j == 1:
                            for g in range(PASSES_1):
                                regroup_pass(1, g)
                        quantise_tokens(j)
                b1_flipped = psum.tile([P, P], BF16, name="b1_flipped", tag="bank")
                nc.tensor.transpose(b1_flipped[:], b1_rows[:], ident_bf[:])
                nc.scalar.copy(out=b1_cols[:], in_=b1_flipped[:])
                for i in range(HEAD_RESIDUALS, TOKEN_TILES):
                    residual(i)

                for n in range(FIRST_PAIR_STEP, H_REGROUP_STEP):
                    if n > 1:
                        regroup_unit(n)
                        quantise_w1_unit(n - 1)
                    for q in range(PAIRS_A_STEP * (n - FIRST_PAIR_STEP), PAIRS_A_STEP * (n - FIRST_PAIR_STEP + 1)):
                        hidden_pair(q)

        with tc.tile_pool(name="late", bufs=3, reuse_waits="tile") as late:
            nc.sync.dma_start(out=gain_bc[:], in_=g2.partition_broadcast(P))
            nc.sync.dma_start(out=shift_bc[:], in_=be2.partition_broadcast(P))

            h_grouped = {}
            h_codes = {}
            h_scales = {}
            ffn = {}
            neg_mean = {}
            rstd = {}
            rows = {}
            centred = {}

            def regroup_hidden(i):
                toks = slice(i * P, (i + 1) * P)
                h_grouped[i] = late.tile([P, PASSES_2, P, PACK], BF16, name="h_grouped", align_bytes=64)
                for g in range(PASSES_2):
                    dst, src = regrouped(h_grouped[i][:, g], hidden[:, PACK * g : PACK * (g + 1), toks], SCALAR_RUN)
                    nc.scalar.copy(out=dst, in_=src)

            def quantise_hidden(i):
                h_codes[i] = late.tile([P, PASSES_2, P], U32, name="h_codes", align_bytes=64)
                h_scales[i] = late.tile([P, PASSES_2, P], U8, name="h_scales", align_bytes=64)
                for g0, g1 in ((0, 4), (4, 6)):
                    nc.vector.quantize_mx(
                        out=h_codes[i][:, g0:g1, :].rearrange("p g w -> p (g w)").bitcast(FP8X4),
                        scales=h_scales[i][:, g0:g1, :].rearrange("p g w -> p (g w)"),
                        in_=h_grouped[i][:, g0:g1].rearrange("p g w t -> p (g w t)"),
                    )

            def second_product(i):
                ffn[i] = []
                for half in range(2):
                    cols = slice(half * BANK, (half + 1) * BANK)
                    acc = psum.tile([P, BANK], F32, name="ffn", tag="bank")
                    ffn[i].append(acc)
                    for g in range(PASSES_2):
                        nc.tensor.matmul_mx(
                            out=acc[:],
                            lhsT=h_codes[i][:, g, :].bitcast(FP8X4),
                            lhsT_scale=h_scales[i][:, g, :],
                            rhs=w2_codes[:, g, cols].bitcast(FP8X4),
                            rhs_scale=w2_scales[:, g, cols],
                            start=(g == 0),
                            stop=(g == PASSES_2 - 1),
                        )

            def add_residual(i):
                r = late.tile([P, D_MODEL], F32, name="r")
                row_sum = late.tile([P, 2], F32, name="row_sum")
                for half in range(2):
                    cols = slice(half * BANK, (half + 1) * BANK)
                    nc.vector.scalar_tensor_tensor(
                        out=r[:, cols],
                        in0=ffn[i][half][:],
                        scalar=0.0,
                        in1=resid[:, i, cols],
                        op0=ALU.add,
                        op1=ALU.add,
                        accum_out=row_sum[:, half : half + 1],
                    )
                neg_mean[i] = late.tile([P, 1], F32, name="neg_mean")
                scaled_sums = late.tile([P, 2], F32, name="scaled_sums")
                nc.scalar.activation(
                    out=scaled_sums[:], in_=row_sum[:], func=ACT.Copy, scale=-1.0 / D_MODEL, accum_out=neg_mean[i][:]
                )
                squares = late.tile([P, D_MODEL], BF16, name="squares", bufs=1)
                sum_sq = late.tile([P, 1], F32, name="sum_sq")
                nc.scalar.activation(
                    out=squares[:], in_=r[:], func=ACT.Square, bias=neg_mean[i][:], scale=1.0, accum_out=sum_sq[:]
                )
                rstd[i] = late.tile([P, 1], F32, name="rstd")
                nc.scalar.activation(
                    out=rstd[i][:], in_=sum_sq[:], func=ACT.Abs_reciprocal_sqrt, bias=eps_col[:], scale=1.0 / D_MODEL
                )
                rows[i] = r

            def centre(i):
                centred[i] = late.tile([P, D_MODEL], F32, name="centred", bufs=2)
                nc.vector.scalar_tensor_tensor(
                    out=centred[i][:], in0=rows[i][:], scalar=neg_mean[i][:], in1=gain_bc[:], op0=ALU.add, op1=ALU.mult
                )

            def scale_and_store(i):
                normed = late.tile([P, D_MODEL], F32, name="normed")
                width = D_MODEL // 2 if i == TOKEN_TILES - 1 else D_MODEL
                for d0 in range(0, D_MODEL, width):
                    cols = slice(d0, d0 + width)
                    nc.vector.scalar_tensor_tensor(
                        out=normed[:, cols],
                        in0=centred[i][:, cols],
                        scalar=rstd[i][:],
                        in1=shift_bc[:, cols],
                        op0=ALU.mult,
                        op1=ALU.add,
                    )
                    nc.sync.dma_start(out=out_rows[i * P : (i + 1) * P, cols], in_=normed[:, cols])

            def early_then_late(first, count, then):
                return [first + i if i < count else then + i - count for i in range(TOKEN_TILES)]

            stages = (
                (early_then_late(H_REGROUP_STEP, EARLY_H, PRODUCT_STEP + EARLY_H - 1), regroup_hidden),
                (early_then_late(H_QUANTISE_STEP, EARLY_H, PRODUCT_STEP + EARLY_H), quantise_hidden),
                (early_then_late(PRODUCT_STEP, TOKEN_TILES, 0), second_product),
                (early_then_late(CENTRE_STEP, TOKEN_TILES, 0), add_residual),
                (early_then_late(STORE_STEP, TOKEN_TILES, 0), scale_and_store),
                (early_then_late(CENTRE_STEP, TOKEN_TILES, 0), centre),
            )
            scalar_grouped = late.tile([P, UNIT_COLS, PACK], BF16, name="scalar_grouped", align_bytes=64, bufs=1)
            grouped_units[SCALAR_UNIT] = scalar_grouped
            for n in range(H_REGROUP_STEP, LAST_STEP + 1):
                if n < SCALAR_UNIT:
                    regroup_unit(n)
                if n - 1 < UNITS:
                    quantise_unit(n - 1, w2_codes[:, n - 1 - W1_UNITS, :], w2_scales[:, n - 1 - W1_UNITS, :])
                for steps, stage in stages:
                    if n in steps:
                        stage(steps.index(n))
                if n == H_REGROUP_STEP:
                    for half in range(2):
                        cols = slice(half * BANK, (half + 1) * BANK)
                        dst, src = regrouped(scalar_grouped[:, cols, :], raw_units[SCALAR_UNIT][:, :, cols], SCALAR_RUN)
                        nc.scalar.copy(out=dst, in_=src)
